import numpy as np
import ml_dtypes


def mxq(x, axis, fmt="e4m3"):
    dtype, down = {"e4m3": (ml_dtypes.float8_e4m3fn, 7), "e5m2": (ml_dtypes.float8_e5m2, 14)}[fmt]
    v = np.moveaxis(np.asarray(x, np.float32).astype(ml_dtypes.bfloat16).astype(np.float64), axis, -1)
    blocks = v.reshape(v.shape[:-1] + (-1, 32))
    amax = np.abs(blocks).max(-1, keepdims=True)
    byte = np.maximum(np.where(amax > 0, np.frexp(amax)[1] - 1 + 127, 0) - down, 1)
    scale = np.exp2(byte - 127.0)
    codes = (blocks / scale).astype(np.float32).astype(dtype).astype(np.float64)
    return np.moveaxis((codes * scale).reshape(v.shape), -1, axis)


WIDE = False


def mx_kscale(k):
    if not WIDE:
        return np.ones(k)
    levels = np.array([10, -10, 5, -5, 0])
    if k % 512:
        return np.exp2(np.random.permutation(np.resize(levels, k // 32))).repeat(32)
    a = np.empty((k // 512, 16))
    for p in range(k // 512):
        a[p, :8] = np.random.permutation(np.resize(levels, 8))
        for g in range(8):
            far = levels[np.abs(levels - a[p, g]) >= 10]
            a[p, g + 8] = far[np.random.randint(len(far))]
    return np.exp2(a.ravel()).repeat(32)


BF16 = ml_dtypes.bfloat16


def bf(x):
    return np.asarray(x, np.float32).astype(BF16)


def f64(x):
    return np.asarray(x).astype(np.float64)


B, C, T, E, H = 1, 48, 128, 512, 4
D = E // H
S = C * T


def heads(y):
    return np.moveaxis(y.reshape(B, C, T, H, D), 3, 1)


def setup_inputs():
    s = mx_kscale(E)
    return {"hidden_states": bf(np.random.standard_normal((B, S, E)) * s),
            "wk": bf(np.random.standard_normal((E, E)) * 2.0 / np.sqrt(E) / s[None, :]),
            "bk": bf(np.random.standard_normal(E) * 0.3),
            "wv": bf(np.random.standard_normal((E, E)) * 2.0 / np.sqrt(E) / s[None, :]),
            "bv": bf(np.random.standard_normal(E) * 0.3)}


def reference(hidden_states, wk, bk, wv, bv):
    xq = mxq(f64(hidden_states), 2, "e4m3")
    k = heads((xq @ mxq(f64(wk), 1, "e4m3").T) + f64(bk))
    v = heads((xq @ mxq(f64(wv), 1, "e4m3").T) + f64(bv))
    return k, v, k.mean(axis=3), v.mean(axis=3)

@@ -1,0 +1,309 @@
+from contextlib import ExitStack
+
+import concourse.mybir as mybir
+from concourse.masks import make_identity
+
+FLOPS = 2 * 6144 * 512 * 1024
+
+F32 = mybir.dt.float32
+BF16 = mybir.dt.bfloat16
+U32 = mybir.dt.uint32
+U8 = mybir.dt.uint8
+FP8X4 = mybir.dt.float8_e4m3fn_x4
+ADD = mybir.AluOpType.add
+MULT = mybir.AluOpType.mult
+
+P = 128
+FAMILIES = 3
+SG_BANKS = (1, 5)
+SG_BANKS_FIRST = (1, 5)
+Q_LAG = 4
+R_LAG = 2
+M_PER_Y = 2
+T_AT = {2: (1, 1), 5: (1, 2), 8: (1, 3), 26: (2, 0), 30: (2, 1), 34: (2, 2), 38: (2, 3)}
+
+
+def tile_chunkedattention_pb_t_kernel(
+    tc, hidden_states, wk, bk, wv, bv, out_0, out_1, out_2, out_3
+):
+    nc = tc.nc
+    with ExitStack() as ctx:
+        const = ctx.enter_context(tc.tile_pool(name="const", bufs=1))
+        stage = ctx.enter_context(tc.tile_pool(name="stage", bufs=3))
+        ypool = ctx.enter_context(tc.tile_pool(name="ypool", bufs=6))
+        psum = ctx.enter_context(tc.psum_pool(name="psum", bufs=2))
+        ctx.enter_context(tc.manual_schedule())
+
+        hs = hidden_states.rearrange("b (g p jh i) e -> (b g) p jh i e", p=P, jh=2, i=8)
+        w_dram = [w.rearrange("(ob p) e -> p ob e", p=P) for w in (wk, wv)]
+        b_dram = [b.rearrange("(o n) -> o n", o=1) for b in (bk, bv)]
+        y_dram = [
+            o.rearrange("b h c t d -> (b h) (c t d)").rearrange("h (g p r) -> g p h r", g=FAMILIES, p=P)
+            for o in (out_0, out_1)
+        ]
+        mean_dram = [o.rearrange("b h c d -> (b h c) d") for o in (out_2, out_3)]
+
+        ident_f = const.tile([P, P], F32, name="ident_f")
+        ident_b = const.tile([P, P], BF16, name="ident_b")
+        ones = const.tile([P, P], BF16, name="ones")
+        bias_in = const.tile([1, 1024], BF16, name="bias_in")
+        bias_row = const.tile([P, 1024], BF16, name="bias_row")
+        bias_bc = const.tile([P, 2, 4, P], F32, name="bias_bc")
+        bcol = const.tile([P, 8], F32, name="bcol")
+        w_sb = [const.tile([P, 4, 512], BF16, name="w_sb%d" % kv) for kv in range(2)]
+        w_codes = [const.tile([P, 512], U32, name="w_codes%d" % kv, align_bytes=64) for kv in range(2)]
+        w_scales = [const.tile([P, 512], U8, name="w_scales%d" % kv, align_bytes=64) for kv in range(2)]
+        x_sb = [const.tile([P, 2, 8, 512], BF16, name="x_sb%d" % g) for g in range(FAMILIES)]
+        x_codes = [const.tile([P, 2048], U32, name="x_codes%d" % g, align_bytes=64) for g in range(FAMILIES)]
+        x_scales = [const.tile([P, 2048], U8, name="x_scales%d" % g, align_bytes=64) for g in range(FAMILIES)]
+        red = const.tile([P, 8, 48], F32, name="red")
+        mean_sb = const.tile([P, 8, 48], F32, name="mean_sb")
+        mt_sb = const.tile([P, 3, P], F32, name="mt_sb")
+
+        state = {"clock": 0, "pending": []}
+
+        def later(lag, fn):
+            state["pending"].append((state["clock"] + lag, fn))
+
+        def tick():
+            state["clock"] += 1
+            due = [x for x in state["pending"] if x[0] <= state["clock"]]
+            state["pending"] = [x for x in state["pending"] if x[0] > state["clock"]]
+            for x in due:
+                x[1]()
+
+        for kv in range(2):
+            nc.scalar.dma_start(out=bias_in[0:1, 512 * kv : 512 * kv + 512], in_=b_dram[kv])
+        nc.vector.memset(bias_row[:], 0.0)
+        nc.vector.memset(ones[:], 1.0)
+        make_identity(nc, ident_f[:])
+        make_identity(nc, ident_b[:])
+
+        def load_x(g, a, b):
+            nc.sync.dma_start(out=x_sb[g][:, :, a:b, :], in_=hs[g][:, :, a:b, :])
+
+        nc.sync.dma_start(out=w_sb[0][:], in_=w_dram[0])
+        load_x(0, 0, 2)
+        load_x(0, 2, 4)
+        load_x(0, 4, 8)
+        nc.sync.dma_start(out=w_sb[1][:], in_=w_dram[1])
+        load_x(1, 0, 4)
+        load_x(1, 4, 8)
+        load_x(2, 0, 4)
+        load_x(2, 4, 8)
+
+        def bias_everywhere(kv, tag, lag):
+            bb_ps = psum.tile([P, 512], F32, name="bb_ps", tag=tag, bufs=(4 if tag == "y" else 2))
+            nc.tensor.matmul(
+                out=bb_ps[:], lhsT=ones[:], rhs=bias_row[:, 512 * kv : 512 * kv + 512], start=True, stop=True
+            )
+            later(
+                lag, lambda: nc.vector.tensor_copy(out=bias_bc[:, kv].rearrange("p h d -> p (h d)"), in_=bb_ps[:])
+            )
+
+        def bias_columns():
+            bc_ps = psum.tile([P, 8, P], BF16, name="bc_ps", tag="y", bufs=4)
+            for fb in range(8):
+                nc.tensor.transpose(bc_ps[:, fb, :], bias_row[:, P * fb : P * fb + P], ident_b[:])
+            later(2, lambda: nc.vector.tensor_copy(out=bcol[:], in_=bc_ps[:, :, 0]))
+
+        def transposed_bank(words, tag):
+            bank = psum.tile([P, 2, 2, P], F32, name="bank_" + tag, tag=tag, bufs=(4 if tag == "y" else 2))
+            for s in range(2):
+                for u in range(2):
+                    nc.tensor.transpose(bank[:, s, u, :], words[s][:, u : 256 : 2], ident_f[:])
+            return bank
+
+        def regroup(engine_copy, grouped, b, bank):
+            view = grouped[:].bitcast(F32).rearrange("q (s t u) -> q s t u", s=4, u=2)
+            engine_copy(out=view[:, 2 * b : 2 * b + 2], in_=bank[:].rearrange("q s u t -> q s t u"))
+
+        def prepare_w(kv, lag):
+            words = w_sb[kv][:].bitcast(F32)
+            grouped = stage.tile([P, 2048], BF16, name="grouped", align_bytes=64)
+            banks = [transposed_bank([words[:, 2 * b + s, :] for s in range(2)], "y") for b in range(2)]
+            regroup(nc.vector.tensor_copy, grouped, 0, banks[0])
+            regroup(nc.scalar.copy, grouped, 1, banks[1])
+            if kv == 0:
+                nc.vector.tensor_copy(out=bias_row[0:1, :], in_=bias_in[:])
+            later(
+                lag,
+                lambda: nc.vector.quantize_mx(
+                    out=w_codes[kv][:].bitcast(FP8X4), scales=w_scales[kv][:], in_=grouped[:]
+                ),
+            )
+
+        def prepare_x(g, rr, lag, share):
+            words = x_sb[g][:].bitcast(F32)
+            grouped = stage.tile([P, 2048], BF16, name="grouped", align_bytes=64)
+            banks = [transposed_bank([words[:, jh, 2 * rr + b, :] for jh in range(2)], "t") for b in range(2)]
+            regroup(nc.scalar.copy, grouped, 0, banks[0])
+            regroup(nc.vector.tensor_copy if share else nc.scalar.copy, grouped, 1, banks[1])
+            cols = slice(512 * rr, 512 * rr + 512)
+
+            def quantise():
+                nc.vector.quantize_mx(
+                    out=x_codes[g][:, cols].bitcast(FP8X4), scales=x_scales[g][:, cols], in_=grouped[:]
+                )
+
+            later(lag, quantise)
+
+        units = {}
+
+        def y_bank(g, kv, hh, i):
+            key = (g, kv, hh)
+            if key not in units:
+                units[key] = ypool.tile([P, 2, 2, 8, P], F32, name="yb")
+            yb = units[key]
+            y_ps = psum.tile([P, 2, 256], F32, name="y_ps", tag="y", bufs=4)
+            feats = slice(256 * hh, 256 * hh + 256)
+            for jh in range(2):
+                toks = slice(P * (2 * i + jh), P * (2 * i + jh) + P)
+                nc.tensor.matmul_mx(
+                    out=y_ps[:, jh, :],
+                    lhsT=x_codes[g][:, toks].bitcast(FP8X4),
+                    lhsT_scale=x_scales[g][:, toks],
+                    rhs=w_codes[kv][:, feats].bitcast(FP8X4),
+                    rhs_scale=w_scales[kv][:, feats],
+                    start=True,
+                    stop=True,
+                )
+            dst = yb[:, :, :, i, :].rearrange("p h jh d -> p jh h d")
+            src = y_ps[:].rearrange("p jh (h d) -> p jh h d", h=2)
+            bias = bias_bc[:, kv, 2 * hh : 2 * hh + 2, :].unsqueeze(1).to_broadcast([P, 2, 2, P])
+            if i in (SG_BANKS_FIRST if key[:2] == (0, 0) else SG_BANKS):
+                nc.scalar.copy(out=dst, in_=src)
+                nc.gpsimd.tensor_tensor(out=dst, in0=dst, in1=bias, op=ADD)
+            else:
+                nc.vector.tensor_tensor(out=dst, in0=src, in1=bias, op=ADD)
+
+        def store_unit(g, kv, hh):
+            yb = units[(g, kv, hh)]
+            nc.sync.dma_start(
+                out=y_dram[kv][g][:, 2 * hh : 2 * hh + 2, :], in_=yb[:].rearrange("p h jh i d -> p h (jh i d)")
+            )
+
+        def store_piece(g, kv, hh, a, b):
+            yb = units[(g, kv, hh)]
+            for h in range(2):
+                nc.sync.dma_start(
+                    out=y_dram[kv][g][:, 2 * hh + h, :].rearrange("p (jh i d) -> p jh i d", jh=2, i=8)[:, :, a:b, :],
+                    in_=yb[:, h, :, a:b, :],
+                )
+
+        m_tiles = {}
+
+        def m_pass(g, fb, i):
+            kv, h = fb // 4, fb % 4
+            if i == 0:
+                m_tiles[(g, fb)] = psum.tile([P, 256], F32, name="m_ps", tag="m")
+            m_ps = m_tiles[(g, fb)]
+            feats = slice(P * h, P * h + P)
+            toks = slice(256 * i, 256 * i + 256)
+            nc.tensor.matmul_mx(
+                out=m_ps[:],
+                lhsT=w_codes[kv][:, feats].bitcast(FP8X4),
+                lhsT_scale=w_scales[kv][:, feats],
+                rhs=x_codes[g][:, toks].bitcast(FP8X4),
+                rhs_scale=x_scales[g][:, toks],
+                start=(i == 0),
+                stop=(i == 7),
+            )
+            if i == 7:
+
+                def reduce_block():
+                    nc.vector.tensor_reduce(
+                        out=red[:, fb, 16 * g : 16 * g + 16],
+                        in_=m_ps[:].rearrange("d (jh c s) -> d c jh s", jh=2, s=8),
+                        axis=mybir.AxisListType.XY,
+                        op=ADD,
+                    )
+                    if g == FAMILIES - 1:
+                        nc.vector.tensor_scalar(
+                            out=mean_sb[:, fb, :],
+                            in0=red[:, fb, :],
+                            scalar1=1.0 / 128.0,
+                            scalar2=bcol[:, fb : fb + 1],
+                            op0=MULT,
+                            op1=ADD,
+                        )
+
+                later(R_LAG, reduce_block)
+
+        def finish_means():
+            mt_ps = psum.tile([P, 3, P], F32, name="mt_ps", tag="t")
+            flat = mean_sb[:].rearrange("d fb c -> d (fb c)")
+            for b in range(3):
+                nc.tensor.transpose(mt_ps[:, b, :], flat[:, P * b : P * b + P], ident_f[:])
+            nc.scalar.copy(out=mt_sb[:], in_=mt_ps[:])
+            nc.sync.dma_start(out=mean_dram[0][0:128, :], in_=mt_sb[:, 0, :])
+            nc.sync.dma_start(out=mean_dram[0][128:192, :], in_=mt_sb[0:64, 1, :])
+            nc.sync.dma_start(out=mean_dram[1][0:64, :], in_=mt_sb[64:128, 1, :])
+            nc.sync.dma_start(out=mean_dram[1][64:192, :], in_=mt_sb[:, 2, :])
+
+        def first_work(rr):
+            for i in (2 * rr, 2 * rr + 1):
+                y_bank(0, 0, 0, i)
+                m_pass(0, 0, i)
+                m_pass(0, 1, i)
+                tick()
+
+        def second_unit(a, b):
+            for i in range(a, b):
+                y_bank(0, 0, 1, i)
+                tick()
+
+        prepare_w(0, 1)
+        tick()
+        prepare_x(0, 0, 1, True)
+        bias_everywhere(0, "m", 1)
+        tick()
+        prepare_x(0, 1, 2, False)
+        tick()
+        first_work(0)
+        prepare_x(0, 2, 3, False)
+        tick()
+        first_work(1)
+        prepare_x(0, 3, 4, False)
+        tick()
+        second_unit(0, 4)
+        first_work(2)
+        first_work(3)
+        store_unit(0, 0, 0)
+        prepare_w(1, 3)
+        bias_everywhere(1, "y", 2)
+        bias_columns()
+        tick()
+        second_unit(4, 6)
+        prepare_x(1, 0, Q_LAG, False)
+        tick()
+        second_unit(6, 8)
+        store_unit(0, 0, 1)
+
+        y_list = [
+            (g, kv, hh, i)
+            for g in range(FAMILIES)
+            for kv in range(2)
+            for hh in range(2)
+            for i in range(8)
+            if (g, kv) != (0, 0)
+        ]
+        m_list = [(g, fb, i) for g in range(FAMILIES) for fb in range(8) for i in range(8) if (g, fb) not in ((0, 0), (0, 1))]
+        m_next = 0
+        for n, (g, kv, hh, i) in enumerate(y_list):
+            if n in T_AT:
+                prepare_x(T_AT[n][0], T_AT[n][1], Q_LAG, False)
+                tick()
+            y_bank(g, kv, hh, i)
+            for m in m_list[m_next : m_next + M_PER_Y]:
+                m_pass(m[0], m[1], m[2])
+            m_next += M_PER_Y
+            tick()
+            if i == 7:
+                store_unit(g, kv, hh)
+        for m in m_list[m_next:]:
+            m_pass(m[0], m[1], m[2])
+            tick()
+        for n in range(8):
+            tick()
+        finish_means()

@@ -11,16 +11,12 @@ U32 = mybir.dt.uint32
 U8 = mybir.dt.uint8
 FP8X4 = mybir.dt.float8_e4m3fn_x4
 ADD = mybir.AluOpType.add
+SUB = mybir.AluOpType.subtract
 MULT = mybir.AluOpType.mult
 
 P = 128
 FAMILIES = 3
-SG_BANKS = (1, 5)
-SG_BANKS_FIRST = (1, 5)
-Q_LAG = 4
-R_LAG = 2
-M_PER_Y = 2
-T_AT = {2: (1, 1), 5: (1, 2), 8: (1, 3), 26: (2, 0), 30: (2, 1), 34: (2, 2), 38: (2, 3)}
+BANKS = 8
 
 
 def tile_chunkedattention_pb_t_kernel(
@@ -34,14 +30,14 @@ def tile_chunkedattention_pb_t_kernel(
         psum = ctx.enter_context(tc.psum_pool(name="psum", bufs=2))
         ctx.enter_context(tc.manual_schedule())
 
-        hs = hidden_states.rearrange("b (g p jh i) e -> (b g) p jh i e", p=P, jh=2, i=8)
+        hs = hidden_states.rearrange("b (g p j) e -> (b g) p j e", p=P, j=16)
         w_dram = [w.rearrange("(ob p) e -> p ob e", p=P) for w in (wk, wv)]
         b_dram = [b.rearrange("(o n) -> o n", o=1) for b in (bk, bv)]
         y_dram = [
             o.rearrange("b h c t d -> (b h) (c t d)").rearrange("h (g p r) -> g p h r", g=FAMILIES, p=P)
             for o in (out_0, out_1)
         ]
-        mean_dram = [o.rearrange("b h c d -> (b h c) d") for o in (out_2, out_3)]
+        mean_dram = [o.rearrange("b h c d -> (b c) h d") for o in (out_2, out_3)]
 
         ident_f = const.tile([P, P], F32, name="ident_f")
         ident_b = const.tile([P, P], BF16, name="ident_b")
@@ -49,16 +45,20 @@ def tile_chunkedattention_pb_t_kernel(
         bias_in = const.tile([1, 1024], BF16, name="bias_in")
         bias_row = const.tile([P, 1024], BF16, name="bias_row")
         bias_bc = const.tile([P, 2, 4, P], F32, name="bias_bc")
-        bcol = const.tile([P, 8], F32, name="bcol")
+        eye_in = const.tile([P, 2048], BF16, name="eye_in", align_bytes=64)
+        eye_codes = const.tile([P, 512], U32, name="eye_codes", align_bytes=64)
+        eye_scales = const.tile([P, 512], U8, name="eye_scales", align_bytes=64)
         w_sb = [const.tile([P, 4, 512], BF16, name="w_sb%d" % kv) for kv in range(2)]
         w_codes = [const.tile([P, 512], U32, name="w_codes%d" % kv, align_bytes=64) for kv in range(2)]
         w_scales = [const.tile([P, 512], U8, name="w_scales%d" % kv, align_bytes=64) for kv in range(2)]
-        x_sb = [const.tile([P, 2, 8, 512], BF16, name="x_sb%d" % g) for g in range(FAMILIES)]
+        wt = [const.tile([P, 4, 512], BF16, name="wt%d" % kv) for kv in range(2)]
+        x_sb = [const.tile([P, 16, 512], BF16, name="x_sb%d" % g) for g in range(FAMILIES)]
         x_codes = [const.tile([P, 2048], U32, name="x_codes%d" % g, align_bytes=64) for g in range(FAMILIES)]
         x_scales = [const.tile([P, 2048], U8, name="x_scales%d" % g, align_bytes=64) for g in range(FAMILIES)]
-        red = const.tile([P, 8, 48], F32, name="red")
-        mean_sb = const.tile([P, 8, 48], F32, name="mean_sb")
-        mt_sb = const.tile([P, 3, P], F32, name="mt_sb")
+        red = const.tile([P, 4, 48], F32, name="red")
+        parts = const.tile([P, 3, 4, P], BF16, name="parts")
+        rest = const.tile([P, 2, 4, 48], F32, name="rest")
+        mean_sb = [const.tile([P, 4, P], F32, name="mean_sb%d" % kv) for kv in range(2)]
 
         state = {"clock": 0, "pending": []}
 
@@ -74,93 +74,71 @@ def tile_chunkedattention_pb_t_kernel(
 
         for kv in range(2):
             nc.scalar.dma_start(out=bias_in[0:1, 512 * kv : 512 * kv + 512], in_=b_dram[kv])
-        nc.vector.memset(bias_row[:], 0.0)
-        nc.vector.memset(ones[:], 1.0)
-        make_identity(nc, ident_f[:])
-        make_identity(nc, ident_b[:])
 
         def load_x(g, a, b):
-            nc.sync.dma_start(out=x_sb[g][:, :, a:b, :], in_=hs[g][:, :, a:b, :])
+            nc.sync.dma_start(out=x_sb[g][:, a:b, :], in_=hs[g][:, a:b, :])
 
         nc.sync.dma_start(out=w_sb[0][:], in_=w_dram[0])
-        load_x(0, 0, 2)
-        load_x(0, 2, 4)
-        load_x(0, 4, 8)
+        for r in range(4):
+            load_x(0, 4 * r, 4 * r + 4)
         nc.sync.dma_start(out=w_sb[1][:], in_=w_dram[1])
-        load_x(1, 0, 4)
-        load_x(1, 4, 8)
-        load_x(2, 0, 4)
-        load_x(2, 4, 8)
+        for g in (1, 2):
+            load_x(g, 0, 8)
+            load_x(g, 8, 16)
 
-        def bias_everywhere(kv, tag, lag):
-            bb_ps = psum.tile([P, 512], F32, name="bb_ps", tag=tag, bufs=(4 if tag == "y" else 2))
+        nc.vector.memset(bias_row[:], 0.0)
+        nc.vector.memset(ones[:], 1.0)
+        nc.vector.memset(eye_in[:], 0.0)
+        make_identity(nc, ident_f[:])
+        make_identity(nc, ident_b[:])
+        for a in range(4):
+            nc.gpsimd.tensor_copy(
+                out=eye_in[:].rearrange("p (q a b) -> p q a b", a=4, b=4)[:, :, a, a], in_=ident_b[:]
+            )
+        nc.gpsimd.memset(parts[:], 0.0)
+
+        def bias_everywhere(kv, lag):
+            bb_ps = psum.tile([P, 512], F32, name="bb_ps", tag="m")
             nc.tensor.matmul(
                 out=bb_ps[:], lhsT=ones[:], rhs=bias_row[:, 512 * kv : 512 * kv + 512], start=True, stop=True
             )
-            later(
-                lag, lambda: nc.vector.tensor_copy(out=bias_bc[:, kv].rearrange("p h d -> p (h d)"), in_=bb_ps[:])
-            )
+            later(lag, lambda: nc.scalar.copy(out=bias_bc[:, kv].rearrange("p h d -> p (h d)"), in_=bb_ps[:]))
 
-        def bias_columns():
-            bc_ps = psum.tile([P, 8, P], BF16, name="bc_ps", tag="y", bufs=4)
-            for fb in range(8):
-                nc.tensor.transpose(bc_ps[:, fb, :], bias_row[:, P * fb : P * fb + P], ident_b[:])
-            later(2, lambda: nc.vector.tensor_copy(out=bcol[:], in_=bc_ps[:, :, 0]))
-
-        def transposed_bank(words, tag):
-            bank = psum.tile([P, 2, 2, P], F32, name="bank_" + tag, tag=tag, bufs=(4 if tag == "y" else 2))
-            for s in range(2):
-                for u in range(2):
-                    nc.tensor.transpose(bank[:, s, u, :], words[s][:, u : 256 : 2], ident_f[:])
-            return bank
-
-        def regroup(engine_copy, grouped, b, bank):
+        def prepare(words, codes, scales, copies, lag):
+            grouped = stage.tile([P, 2048], BF16, name="grouped", align_bytes=64)
             view = grouped[:].bitcast(F32).rearrange("q (s t u) -> q s t u", s=4, u=2)
-            engine_copy(out=view[:, 2 * b : 2 * b + 2], in_=bank[:].rearrange("q s u t -> q s t u"))
+            for b in range(2):
+                bank = psum.tile([P, 2, 2, P], F32, name="bank", tag="t")
+                for s in range(2):
+                    for u in range(2):
+                        nc.tensor.transpose(bank[:, s, u, :], words[2 * b + s][:, u : 256 : 2], ident_f[:])
+                copies[b](out=view[:, 2 * b : 2 * b + 2], in_=bank[:].rearrange("q s u t -> q s t u"))
+            later(lag, lambda: nc.vector.quantize_mx(out=codes.bitcast(FP8X4), scales=scales, in_=grouped[:]))
 
-        def prepare_w(kv, lag):
+        def prepare_w(kv, copies, lag):
             words = w_sb[kv][:].bitcast(F32)
-            grouped = stage.tile([P, 2048], BF16, name="grouped", align_bytes=64)
-            banks = [transposed_bank([words[:, 2 * b + s, :] for s in range(2)], "y") for b in range(2)]
-            regroup(nc.vector.tensor_copy, grouped, 0, banks[0])
-            regroup(nc.scalar.copy, grouped, 1, banks[1])
-            if kv == 0:
-                nc.vector.tensor_copy(out=bias_row[0:1, :], in_=bias_in[:])
-            later(
-                lag,
-                lambda: nc.vector.quantize_mx(
-                    out=w_codes[kv][:].bitcast(FP8X4), scales=w_scales[kv][:], in_=grouped[:]
-                ),
-            )
+            prepare([words[:, ob, :] for ob in range(4)], w_codes[kv][:], w_scales[kv][:], copies, lag)
 
-        def prepare_x(g, rr, lag, share):
+        def prepare_x(g, r, copies, lag):
             words = x_sb[g][:].bitcast(F32)
-            grouped = stage.tile([P, 2048], BF16, name="grouped", align_bytes=64)
-            banks = [transposed_bank([words[:, jh, 2 * rr + b, :] for jh in range(2)], "t") for b in range(2)]
-            regroup(nc.scalar.copy, grouped, 0, banks[0])
-            regroup(nc.vector.tensor_copy if share else nc.scalar.copy, grouped, 1, banks[1])
-            cols = slice(512 * rr, 512 * rr + 512)
+            cols = slice(512 * r, 512 * r + 512)
+            prepare([words[:, 4 * r + s, :] for s in range(4)], x_codes[g][:, cols], x_scales[g][:, cols], copies, lag)
 
-            def quantise():
-                nc.vector.quantize_mx(
-                    out=x_codes[g][:, cols].bitcast(FP8X4), scales=x_scales[g][:, cols], in_=grouped[:]
-                )
-
-            later(lag, quantise)
+        SS = (nc.scalar.copy, nc.scalar.copy)
+        SV = (nc.scalar.copy, nc.vector.tensor_copy)
 
         units = {}
 
-        def y_bank(g, kv, hh, i):
+        def y_bank(g, kv, hh, b, on_scalar):
             key = (g, kv, hh)
             if key not in units:
-                units[key] = ypool.tile([P, 2, 2, 8, P], F32, name="yb")
-            yb = units[key]
+                units[key] = ypool.tile([P, 2, 16, P], F32, name="yb")
             y_ps = psum.tile([P, 2, 256], F32, name="y_ps", tag="y", bufs=4)
             feats = slice(256 * hh, 256 * hh + 256)
-            for jh in range(2):
-                toks = slice(P * (2 * i + jh), P * (2 * i + jh) + P)
+            for s in range(2):
+                toks = slice(P * (2 * b + s), P * (2 * b + s) + P)
                 nc.tensor.matmul_mx(
-                    out=y_ps[:, jh, :],
+                    out=y_ps[:, s, :],
                     lhsT=x_codes[g][:, toks].bitcast(FP8X4),
                     lhsT_scale=x_scales[g][:, toks],
                     rhs=w_codes[kv][:, feats].bitcast(FP8X4),
@@ -168,142 +146,148 @@ def tile_chunkedattention_pb_t_kernel(
                     start=True,
                     stop=True,
                 )
-            dst = yb[:, :, :, i, :].rearrange("p h jh d -> p jh h d")
-            src = y_ps[:].rearrange("p jh (h d) -> p jh h d", h=2)
+            dst = units[key][:, :, 2 * b : 2 * b + 2, :].rearrange("p h j d -> p j h d")
+            src = y_ps[:].rearrange("p j (h d) -> p j h d", h=2)
             bias = bias_bc[:, kv, 2 * hh : 2 * hh + 2, :].unsqueeze(1).to_broadcast([P, 2, 2, P])
-            if i in (SG_BANKS_FIRST if key[:2] == (0, 0) else SG_BANKS):
+            if on_scalar:
                 nc.scalar.copy(out=dst, in_=src)
                 nc.gpsimd.tensor_tensor(out=dst, in0=dst, in1=bias, op=ADD)
             else:
                 nc.vector.tensor_tensor(out=dst, in0=src, in1=bias, op=ADD)
 
-        def store_unit(g, kv, hh):
-            yb = units[(g, kv, hh)]
+        def store(g, kv, hh, a, b):
             nc.sync.dma_start(
-                out=y_dram[kv][g][:, 2 * hh : 2 * hh + 2, :], in_=yb[:].rearrange("p h jh i d -> p h (jh i d)")
+                out=y_dram[kv][g][:, 2 * hh : 2 * hh + 2, :].rearrange("p h (j d) -> p h j d", d=P)[:, :, a:b, :],
+                in_=units[(g, kv, hh)][:, :, a:b, :],
             )
-
-        def store_piece(g, kv, hh, a, b):
-            yb = units[(g, kv, hh)]
-            for h in range(2):
-                nc.sync.dma_start(
-                    out=y_dram[kv][g][:, 2 * hh + h, :].rearrange("p (jh i d) -> p jh i d", jh=2, i=8)[:, :, a:b, :],
-                    in_=yb[:, h, :, a:b, :],
-                )
 
         m_tiles = {}
 
-        def m_pass(g, fb, i):
-            kv, h = fb // 4, fb % 4
-            if i == 0:
-                m_tiles[(g, fb)] = psum.tile([P, 256], F32, name="m_ps", tag="m")
-            m_ps = m_tiles[(g, fb)]
-            feats = slice(P * h, P * h + P)
-            toks = slice(256 * i, 256 * i + 256)
+        def quantise_eye():
+            nc.vector.quantize_mx(out=eye_codes[:].bitcast(FP8X4), scales=eye_scales[:], in_=eye_in[:])
+
+        def m_pass(g, kb, q):
+            if q == 0:
+                m_tiles[(g, kb)] = psum.tile([P, 256], F32, name="m_ps", tag="m")
+            m_ps = m_tiles[(g, kb)]
+            toks = slice(256 * q, 256 * q + 256)
+            ks = slice(P * kb, P * kb + P)
             nc.tensor.matmul_mx(
                 out=m_ps[:],
-                lhsT=w_codes[kv][:, feats].bitcast(FP8X4),
-                lhsT_scale=w_scales[kv][:, feats],
+                lhsT=eye_codes[:, ks].bitcast(FP8X4),
+                lhsT_scale=eye_scales[:, ks],
                 rhs=x_codes[g][:, toks].bitcast(FP8X4),
                 rhs_scale=x_scales[g][:, toks],
-                start=(i == 0),
-                stop=(i == 7),
+                start=(q == 0),
+                stop=(q == 7),
             )
-            if i == 7:
-
-                def reduce_block():
-                    nc.vector.tensor_reduce(
-                        out=red[:, fb, 16 * g : 16 * g + 16],
-                        in_=m_ps[:].rearrange("d (jh c s) -> d c jh s", jh=2, s=8),
+            if q == 7:
+                later(
+                    2,
+                    lambda: nc.vector.tensor_reduce(
+                        out=red[:, kb, 16 * g : 16 * g + 16],
+                        in_=m_ps[:].rearrange("d (s c p) -> d c s p", s=2, p=8),
                         axis=mybir.AxisListType.XY,
                         op=ADD,
+                    ),
+                )
+
+        def weight_back(kv, kb):
+            ks = slice(P * kb, P * kb + P)
+            wt_ps = psum.tile([P, 512], F32, name="wt_ps", tag="t")
+            nc.tensor.matmul_mx(
+                out=wt_ps[:],
+                lhsT=eye_codes[:, ks].bitcast(FP8X4),
+                lhsT_scale=eye_scales[:, ks],
+                rhs=w_codes[kv][:].bitcast(FP8X4),
+                rhs_scale=w_scales[kv][:],
+                start=True,
+                stop=True,
+            )
+            later(1, lambda: nc.scalar.copy(out=wt[kv][:, kb, :], in_=wt_ps[:]))
+
+        def split_sums():
+            nc.vector.tensor_copy(out=parts[:, 0, :, 0:48], in_=red[:])
+            nc.vector.tensor_tensor(out=rest[:, 0], in0=red[:], in1=parts[:, 0, :, 0:48], op=SUB)
+            nc.vector.tensor_copy(out=parts[:, 1, :, 0:48], in_=rest[:, 0])
+            nc.vector.tensor_tensor(out=rest[:, 1], in0=rest[:, 0], in1=parts[:, 1, :, 0:48], op=SUB)
+            nc.vector.tensor_copy(out=parts[:, 2, :, 0:48], in_=rest[:, 1])
+
+        def f_pass(kv, n):
+            if n == 0:
+                m_tiles[kv] = psum.tile([P, 512], F32, name="f_ps", tag="t")
+            f_ps = m_tiles[kv]
+            nc.tensor.matmul(
+                out=f_ps[:], lhsT=parts[:, n // 4, n % 4, :], rhs=wt[kv][:, n % 4, :], start=(n == 0), stop=(n == 11)
+            )
+            if n == 11:
+
+                def finish():
+                    nc.vector.scalar_tensor_tensor(
+                        out=mean_sb[kv][0:48].rearrange("c h d -> c (h d)"),
+                        in0=f_ps[0:48, :],
+                        scalar=1.0 / 128.0,
+                        in1=bias_bc[0:48, kv].rearrange("c h d -> c (h d)"),
+                        op0=MULT,
+                        op1=ADD,
                     )
-                    if g == FAMILIES - 1:
-                        nc.vector.tensor_scalar(
-                            out=mean_sb[:, fb, :],
-                            in0=red[:, fb, :],
-                            scalar1=1.0 / 128.0,
-                            scalar2=bcol[:, fb : fb + 1],
-                            op0=MULT,
-                            op1=ADD,
-                        )
+                    nc.sync.dma_start(out=mean_dram[kv], in_=mean_sb[kv][0:48])
 
-                later(R_LAG, reduce_block)
+                later(1, finish)
 
-        def finish_means():
-            mt_ps = psum.tile([P, 3, P], F32, name="mt_ps", tag="t")
-            flat = mean_sb[:].rearrange("d fb c -> d (fb c)")
-            for b in range(3):
-                nc.tensor.transpose(mt_ps[:, b, :], flat[:, P * b : P * b + P], ident_f[:])
-            nc.scalar.copy(out=mt_sb[:], in_=mt_ps[:])
-            nc.sync.dma_start(out=mean_dram[0][0:128, :], in_=mt_sb[:, 0, :])
-            nc.sync.dma_start(out=mean_dram[0][128:192, :], in_=mt_sb[0:64, 1, :])
-            nc.sync.dma_start(out=mean_dram[1][0:64, :], in_=mt_sb[64:128, 1, :])
-            nc.sync.dma_start(out=mean_dram[1][64:192, :], in_=mt_sb[:, 2, :])
+        def bank(n):
+            u, b = n // BANKS, n % BANKS
+            y_bank(u // 4, u // 2 % 2, u % 2, b, (0, 0, 1, 0, 0, 1, 0, 1 if u % 2 and u > 1 else 0)[b])
+            if b == 3 or b == 7:
+                store(u // 4, u // 2 % 2, u % 2, 2 * b - 6, 2 * b + 2)
 
-        def first_work(rr):
-            for i in (2 * rr, 2 * rr + 1):
-                y_bank(0, 0, 0, i)
-                m_pass(0, 0, i)
-                m_pass(0, 1, i)
-                tick()
+        prepare_w(0, SV, 1)
+        tick()
+        prepare_x(0, 0, SV, 1)
+        nc.vector.tensor_copy(out=bias_row[0:1, :], in_=bias_in[:])
+        bias_everywhere(0, 1)
+        tick()
+        prepare_x(0, 1, SV, 1)
+        bias_everywhere(1, 1)
+        tick()
+        quantise_eye()
+        bank(0)
+        bank(1)
+        prepare_x(0, 2, SS, 1)
+        tick()
+        bank(2)
+        bank(3)
+        prepare_x(0, 3, SS, 1)
+        tick()
 
-        def second_unit(a, b):
-            for i in range(a, b):
-                y_bank(0, 0, 1, i)
-                tick()
-
-        prepare_w(0, 1)
-        tick()
-        prepare_x(0, 0, 1, True)
-        bias_everywhere(0, "m", 1)
-        tick()
-        prepare_x(0, 1, 2, False)
-        tick()
-        first_work(0)
-        prepare_x(0, 2, 3, False)
-        tick()
-        first_work(1)
-        prepare_x(0, 3, 4, False)
-        tick()
-        second_unit(0, 4)
-        first_work(2)
-        first_work(3)
-        store_unit(0, 0, 0)
-        prepare_w(1, 3)
-        bias_everywhere(1, "y", 2)
-        bias_columns()
-        tick()
-        second_unit(4, 6)
-        prepare_x(1, 0, Q_LAG, False)
-        tick()
-        second_unit(6, 8)
-        store_unit(0, 0, 1)
-
-        y_list = [
-            (g, kv, hh, i)
-            for g in range(FAMILIES)
-            for kv in range(2)
-            for hh in range(2)
-            for i in range(8)
-            if (g, kv) != (0, 0)
-        ]
-        m_list = [(g, fb, i) for g in range(FAMILIES) for fb in range(8) for i in range(8) if (g, fb) not in ((0, 0), (0, 1))]
-        m_next = 0
-        for n, (g, kv, hh, i) in enumerate(y_list):
-            if n in T_AT:
-                prepare_x(T_AT[n][0], T_AT[n][1], Q_LAG, False)
-                tick()
-            y_bank(g, kv, hh, i)
-            for m in m_list[m_next : m_next + M_PER_Y]:
-                m_pass(m[0], m[1], m[2])
-            m_next += M_PER_Y
+        preps = {5: (1, 0), 13: (1, 1), 17: (1, 2), 22: (1, 3), 30: (2, 0), 36: (2, 1), 42: (2, 2), 48: (2, 3)}
+        m_list = [(g, kb, q) for g in range(FAMILIES) for kb in range(4) for q in range(8)]
+        f_list = [(kv, n) for kv in range(2) for n in range(12)]
+        wb_list = [(kv, kb) for kv in range(2) for kb in range(4)]
+        for n in range(4, 12 * BANKS):
+            if n == 9:
+                prepare_w(1, SS, 3)
+            elif n in preps:
+                prepare_x(preps[n][0], preps[n][1], SS, 3)
+            bank(n)
+            if n >= 10:
+                ready = 32 if n < 27 else 64 if n < 53 else 96
+                take = 1 if n < 48 else 2
+                while take and m_list and 96 - len(m_list) < ready:
+                    m_pass(*m_list[0])
+                    m_list = m_list[1:]
+                    take -= 1
+            if n >= 54 and n % 3 == 0 and wb_list:
+                weight_back(*wb_list[0])
+                wb_list = wb_list[1:]
             tick()
-            if i == 7:
-                store_unit(g, kv, hh)
-        for m in m_list[m_next:]:
-            m_pass(m[0], m[1], m[2])
+            if n == 81:
+                split_sums()
+            if n >= 83:
+                for f in f_list[0:2]:
+                    f_pass(f[0], f[1])
+                f_list = f_list[2:]
+        for f in f_list:
+            f_pass(f[0], f[1])
+        for n in range(4):
             tick()
-        for n in range(8):
-            tick()
-        finish_means()

@@ -16,6 +16,9 @@ MULT = mybir.AluOpType.mult
 
 P = 128
 FAMILIES = 3
+Y_BUFS = 4
+T_BUFS = 2
+M_BUFS = 2
 BANKS = 8
 
 
@@ -26,7 +29,7 @@ def tile_chunkedattention_pb_t_kernel(
     with ExitStack() as ctx:
         const = ctx.enter_context(tc.tile_pool(name="const", bufs=1))
         stage = ctx.enter_context(tc.tile_pool(name="stage", bufs=3))
-        ypool = ctx.enter_context(tc.tile_pool(name="ypool", bufs=6))
+        ypool = ctx.enter_context(tc.tile_pool(name="ypool", bufs=5))
         psum = ctx.enter_context(tc.psum_pool(name="psum", bufs=2))
         ctx.enter_context(tc.manual_schedule())
 
@@ -56,7 +59,8 @@ def tile_chunkedattention_pb_t_kernel(
         x_codes = [const.tile([P, 2048], U32, name="x_codes%d" % g, align_bytes=64) for g in range(FAMILIES)]
         x_scales = [const.tile([P, 2048], U8, name="x_scales%d" % g, align_bytes=64) for g in range(FAMILIES)]
         red = const.tile([P, 4, 48], F32, name="red")
-        parts = const.tile([P, 3, 4, P], BF16, name="parts")
+        parts = const.tile([P, 4, 3, 48], BF16, name="parts")
+        sums = const.tile([P, 8, P], F32, name="sums")
         rest = const.tile([P, 2, 4, 48], F32, name="rest")
         mean_sb = [const.tile([P, 4, P], F32, name="mean_sb%d" % kv) for kv in range(2)]
 
@@ -95,34 +99,54 @@ def tile_chunkedattention_pb_t_kernel(
             nc.gpsimd.tensor_copy(
                 out=eye_in[:].rearrange("p (q a b) -> p q a b", a=4, b=4)[:, :, a, a], in_=ident_b[:]
             )
-        nc.gpsimd.memset(parts[:], 0.0)
+        nc.gpsimd.memset(sums[:], 0.0)
 
         def bias_everywhere(kv, lag):
-            bb_ps = psum.tile([P, 512], F32, name="bb_ps", tag="m")
+            bb_ps = psum.tile([P, 512], F32, name="bb_ps", tag="m", bufs=M_BUFS)
             nc.tensor.matmul(
                 out=bb_ps[:], lhsT=ones[:], rhs=bias_row[:, 512 * kv : 512 * kv + 512], start=True, stop=True
             )
             later(lag, lambda: nc.scalar.copy(out=bias_bc[:, kv].rearrange("p h d -> p (h d)"), in_=bb_ps[:]))
 
-        def prepare(words, codes, scales, copies, lag):
+        def prepare(words, codes, scales, copies, lag, tag="t"):
             grouped = stage.tile([P, 2048], BF16, name="grouped", align_bytes=64)
             view = grouped[:].bitcast(F32).rearrange("q (s t u) -> q s t u", s=4, u=2)
             for b in range(2):
-                bank = psum.tile([P, 2, 2, P], F32, name="bank", tag="t")
+                bank = psum.tile([P, 2, 2, P], F32, name="bank", tag=tag, bufs=T_BUFS if tag == "t" else Y_BUFS)
                 for s in range(2):
                     for u in range(2):
-                        nc.tensor.transpose(bank[:, s, u, :], words[2 * b + s][:, u : 256 : 2], ident_f[:])
+                        nc.tensor.transpose(bank[:, s, u, :], words(2 * b + s, u), ident_f[:])
                 copies[b](out=view[:, 2 * b : 2 * b + 2], in_=bank[:].rearrange("q s u t -> q s t u"))
             later(lag, lambda: nc.vector.quantize_mx(out=codes.bitcast(FP8X4), scales=scales, in_=grouped[:]))
 
-        def prepare_w(kv, copies, lag):
+        def prepare_w(kv, copies, lag, tag="t"):
             words = w_sb[kv][:].bitcast(F32)
-            prepare([words[:, ob, :] for ob in range(4)], w_codes[kv][:], w_scales[kv][:], copies, lag)
+            prepare(lambda s, u: words[:, s, u : 256 : 2], w_codes[kv][:], w_scales[kv][:], copies, lag, tag)
 
-        def prepare_x(g, r, copies, lag):
+        def prepare_x(g, r, copies, lag, tag="t"):
             words = x_sb[g][:].bitcast(F32)
             cols = slice(512 * r, 512 * r + 512)
-            prepare([words[:, 4 * r + s, :] for s in range(4)], x_codes[g][:, cols], x_scales[g][:, cols], copies, lag)
+            if (g, r) in sorted_words:
+                words = sorted_words[(g, r)]
+                prepare(lambda s, u: words[:, s, u, :], x_codes[g][:, cols], x_scales[g][:, cols], copies, lag, tag)
+            else:
+                prepare(
+                    lambda s, u: words[:, 4 * r + s, u : 256 : 2],
+                    x_codes[g][:, cols],
+                    x_scales[g][:, cols],
+                    copies,
+                    lag,
+                    tag,
+                )
+
+        sorted_words = {}
+
+        def sort_words(g, r):
+            t = stage.tile([P, 4, 2, P], F32, name="sorted", bufs=2)
+            sorted_words[(g, r)] = t
+            nc.scalar.copy(
+                out=t[:], in_=x_sb[g][:].bitcast(F32)[:, 4 * r : 4 * r + 4, :].rearrange("p s (q u) -> p s u q", u=2)
+            )
 
         SS = (nc.scalar.copy, nc.scalar.copy)
         SV = (nc.scalar.copy, nc.vector.tensor_copy)
@@ -133,7 +157,7 @@ def tile_chunkedattention_pb_t_kernel(
             key = (g, kv, hh)
             if key not in units:
                 units[key] = ypool.tile([P, 2, 16, P], F32, name="yb")
-            y_ps = psum.tile([P, 2, 256], F32, name="y_ps", tag="y", bufs=4)
+            y_ps = psum.tile([P, 2, 256], F32, name="y_ps", tag="y", bufs=Y_BUFS)
             feats = slice(256 * hh, 256 * hh + 256)
             for s in range(2):
                 toks = slice(P * (2 * b + s), P * (2 * b + s) + P)
@@ -168,7 +192,7 @@ def tile_chunkedattention_pb_t_kernel(
 
         def m_pass(g, kb, q):
             if q == 0:
-                m_tiles[(g, kb)] = psum.tile([P, 256], F32, name="m_ps", tag="m")
+                m_tiles[(g, kb)] = psum.tile([P, 256], F32, name="m_ps", tag="m", bufs=M_BUFS)
             m_ps = m_tiles[(g, kb)]
             toks = slice(256 * q, 256 * q + 256)
             ks = slice(P * kb, P * kb + P)
@@ -183,7 +207,7 @@ def tile_chunkedattention_pb_t_kernel(
             )
             if q == 7:
                 later(
-                    2,
+                    1,
                     lambda: nc.vector.tensor_reduce(
                         out=red[:, kb, 16 * g : 16 * g + 16],
                         in_=m_ps[:].rearrange("d (s c p) -> d c s p", s=2, p=8),
@@ -194,7 +218,7 @@ def tile_chunkedattention_pb_t_kernel(
 
         def weight_back(kv, kb):
             ks = slice(P * kb, P * kb + P)
-            wt_ps = psum.tile([P, 512], F32, name="wt_ps", tag="t")
+            wt_ps = psum.tile([P, 512], F32, name="wt_ps", tag="t", bufs=T_BUFS)
             nc.tensor.matmul_mx(
                 out=wt_ps[:],
                 lhsT=eye_codes[:, ks].bitcast(FP8X4),
@@ -207,47 +231,58 @@ def tile_chunkedattention_pb_t_kernel(
             later(1, lambda: nc.scalar.copy(out=wt[kv][:, kb, :], in_=wt_ps[:]))
 
         def split_sums():
-            nc.vector.tensor_copy(out=parts[:, 0, :, 0:48], in_=red[:])
-            nc.vector.tensor_tensor(out=rest[:, 0], in0=red[:], in1=parts[:, 0, :, 0:48], op=SUB)
-            nc.vector.tensor_copy(out=parts[:, 1, :, 0:48], in_=rest[:, 0])
-            nc.vector.tensor_tensor(out=rest[:, 1], in0=rest[:, 0], in1=parts[:, 1, :, 0:48], op=SUB)
-            nc.vector.tensor_copy(out=parts[:, 2, :, 0:48], in_=rest[:, 1])
+            nc.vector.tensor_copy(out=parts[:, :, 0, :], in_=red[:])
+            nc.vector.tensor_tensor(out=rest[:, 0], in0=red[:], in1=parts[:, :, 0, :], op=SUB)
+            nc.vector.tensor_copy(out=parts[:, :, 1, :], in_=rest[:, 0])
+            nc.vector.tensor_tensor(out=rest[:, 1], in0=rest[:, 0], in1=parts[:, :, 1, :], op=SUB)
+            nc.vector.tensor_copy(out=parts[:, :, 2, :], in_=rest[:, 1])
 
-        def f_pass(kv, n):
-            if n == 0:
-                m_tiles[kv] = psum.tile([P, 512], F32, name="f_ps", tag="t")
-            f_ps = m_tiles[kv]
-            nc.tensor.matmul(
-                out=f_ps[:], lhsT=parts[:, n // 4, n % 4, :], rhs=wt[kv][:, n % 4, :], start=(n == 0), stop=(n == 11)
-            )
-            if n == 11:
+        def f_block(fb):
+            if fb == 0:
+                m_tiles["f"] = psum.tile([P, 8, 48], F32, name="f_ps", tag="m", bufs=M_BUFS)
+            f_ps = m_tiles["f"]
+            for n in range(12):
+                nc.tensor.matmul(
+                    out=f_ps[:, fb, :],
+                    lhsT=wt[fb // 4][:, n % 4, P * (fb % 4) : P * (fb % 4) + P],
+                    rhs=parts[:, n % 4, n // 4, :],
+                    start=(n == 0),
+                    stop=(n == 11),
+                )
+            if fb == 7:
+                later(1, lambda: nc.scalar.copy(out=sums[:, :, 0:48], in_=f_ps[:]))
 
-                def finish():
-                    nc.vector.scalar_tensor_tensor(
-                        out=mean_sb[kv][0:48].rearrange("c h d -> c (h d)"),
-                        in0=f_ps[0:48, :],
-                        scalar=1.0 / 128.0,
-                        in1=bias_bc[0:48, kv].rearrange("c h d -> c (h d)"),
-                        op0=MULT,
-                        op1=ADD,
-                    )
-                    nc.sync.dma_start(out=mean_dram[kv], in_=mean_sb[kv][0:48])
+        def means_out(kv):
+            t_ps = psum.tile([P, 4, P], F32, name="t_ps", tag="t", bufs=T_BUFS)
+            for h in range(4):
+                nc.tensor.transpose(t_ps[:, h, :], sums[:, 4 * kv + h, :], ident_f[:])
 
-                later(1, finish)
+            def finish():
+                nc.vector.scalar_tensor_tensor(
+                    out=mean_sb[kv][0:48].rearrange("c h d -> c (h d)"),
+                    in0=t_ps[0:48].rearrange("c h d -> c (h d)"),
+                    scalar=1.0 / 128.0,
+                    in1=bias_bc[0:48, kv].rearrange("c h d -> c (h d)"),
+                    op0=MULT,
+                    op1=ADD,
+                )
+                nc.sync.dma_start(out=mean_dram[kv], in_=mean_sb[kv][0:48])
+
+            later(1, finish)
 
         def bank(n):
             u, b = n // BANKS, n % BANKS
-            y_bank(u // 4, u // 2 % 2, u % 2, b, (0, 0, 1, 0, 0, 1, 0, 1 if u % 2 and u > 1 else 0)[b])
-            if b == 3 or b == 7:
-                store(u // 4, u // 2 % 2, u % 2, 2 * b - 6, 2 * b + 2)
+            y_bank(u // 4, u // 2 % 2, u % 2, b, b in (2, 6))
+            for a, c in {3: ((0, 8),), 7: ((8, 16),)}.get(b, ()):
+                store(u // 4, u // 2 % 2, u % 2, a, c)
 
-        prepare_w(0, SV, 1)
+        nc.vector.tensor_copy(out=bias_row[0:1, :], in_=bias_in[:])
+        prepare_w(0, SV, 1, "y")
         tick()
         prepare_x(0, 0, SV, 1)
-        nc.vector.tensor_copy(out=bias_row[0:1, :], in_=bias_in[:])
-        bias_everywhere(0, 1)
         tick()
-        prepare_x(0, 1, SV, 1)
+        prepare_x(0, 1, SV, 1, "y")
+        bias_everywhere(0, 1)
         bias_everywhere(1, 1)
         tick()
         quantise_eye()
@@ -260,34 +295,37 @@ def tile_chunkedattention_pb_t_kernel(
         prepare_x(0, 3, SS, 1)
         tick()
 
-        preps = {5: (1, 0), 13: (1, 1), 17: (1, 2), 22: (1, 3), 30: (2, 0), 36: (2, 1), 42: (2, 2), 48: (2, 3)}
+        preps = {5: (1, 0), 13: (1, 1), 17: (1, 2), 21: (1, 3), 30: (2, 0), 36: (2, 1), 42: (2, 2), 48: (2, 3)}
         m_list = [(g, kb, q) for g in range(FAMILIES) for kb in range(4) for q in range(8)]
-        f_list = [(kv, n) for kv in range(2) for n in range(12)]
         wb_list = [(kv, kb) for kv in range(2) for kb in range(4)]
+        pause = 0
         for n in range(4, 12 * BANKS):
+            if n + 3 in preps and preps[n + 3] in ():
+                sort_words(*preps[n + 3])
             if n == 9:
                 prepare_w(1, SS, 3)
             elif n in preps:
-                prepare_x(preps[n][0], preps[n][1], SS, 3)
+                prepare_x(preps[n][0], preps[n][1], SS, 5)
             bank(n)
             if n >= 10:
-                ready = 32 if n < 27 else 64 if n < 53 else 96
+                ready = 32 if n < 30 else 64 if n < 56 else 96
                 take = 1 if n < 48 else 2
-                while take and m_list and 96 - len(m_list) < ready:
+                while take and m_list and 96 - len(m_list) < ready and n >= pause:
                     m_pass(*m_list[0])
                     m_list = m_list[1:]
                     take -= 1
+                    if len(m_list) % 8 == 0:
+                        pause = n + 0
             if n >= 54 and n % 3 == 0 and wb_list:
                 weight_back(*wb_list[0])
                 wb_list = wb_list[1:]
             tick()
             if n == 81:
                 split_sums()
-            if n >= 83:
-                for f in f_list[0:2]:
-                    f_pass(f[0], f[1])
-                f_list = f_list[2:]
-        for f in f_list:
-            f_pass(f[0], f[1])
+            if 81 + 3 <= n < 81 + 7:
+                f_block(2 * (n - 81 - 3))
+                f_block(2 * (n - 81 - 3) + 1)
+            if n in (81 + 9, 81 + 11):
+                means_out((n - 81 - 9) // 2)
         for n in range(4):
             tick()

@@ -108,7 +108,13 @@ def tile_chunkedattention_pb_t_kernel(
             )
             later(lag, lambda: nc.scalar.copy(out=bias_bc[:, kv].rearrange("p h d -> p (h d)"), in_=bb_ps[:]))
 
-        def prepare(words, codes, scales, copies, lag, tag="t"):
+        waiting = []
+
+        def quantise_next():
+            waiting[0]()
+            waiting.remove(waiting[0])
+
+        def prepare(words, codes, scales, copies, tag="t"):
             grouped = stage.tile([P, 2048], BF16, name="grouped", align_bytes=64)
             view = grouped[:].bitcast(F32).rearrange("q (s t u) -> q s t u", s=4, u=2)
             for b in range(2):
@@ -117,25 +123,24 @@ def tile_chunkedattention_pb_t_kernel(
                     for u in range(2):
                         nc.tensor.transpose(bank[:, s, u, :], words(2 * b + s, u), ident_f[:])
                 copies[b](out=view[:, 2 * b : 2 * b + 2], in_=bank[:].rearrange("q s u t -> q s t u"))
-            later(lag, lambda: nc.vector.quantize_mx(out=codes.bitcast(FP8X4), scales=scales, in_=grouped[:]))
+            waiting.append(lambda: nc.vector.quantize_mx(out=codes.bitcast(FP8X4), scales=scales, in_=grouped[:]))
 
-        def prepare_w(kv, copies, lag, tag="t"):
+        def prepare_w(kv, copies, tag="t"):
             words = w_sb[kv][:].bitcast(F32)
-            prepare(lambda s, u: words[:, s, u : 256 : 2], w_codes[kv][:], w_scales[kv][:], copies, lag, tag)
+            prepare(lambda s, u: words[:, s, u : 256 : 2], w_codes[kv][:], w_scales[kv][:], copies, tag)
 
-        def prepare_x(g, r, copies, lag, tag="t"):
+        def prepare_x(g, r, copies, tag="t"):
             words = x_sb[g][:].bitcast(F32)
             cols = slice(512 * r, 512 * r + 512)
             if (g, r) in sorted_words:
                 words = sorted_words[(g, r)]
-                prepare(lambda s, u: words[:, s, u, :], x_codes[g][:, cols], x_scales[g][:, cols], copies, lag, tag)
+                prepare(lambda s, u: words[:, s, u, :], x_codes[g][:, cols], x_scales[g][:, cols], copies, tag)
             else:
                 prepare(
                     lambda s, u: words[:, 4 * r + s, u : 256 : 2],
                     x_codes[g][:, cols],
                     x_scales[g][:, cols],
                     copies,
-                    lag,
                     tag,
                 )
 
@@ -272,60 +277,59 @@ def tile_chunkedattention_pb_t_kernel(
 
         def bank(n):
             u, b = n // BANKS, n % BANKS
-            y_bank(u // 4, u // 2 % 2, u % 2, b, b in (2, 6))
-            for a, c in {3: ((0, 8),), 7: ((8, 16),)}.get(b, ()):
+            y_bank(u // 4, u // 2 % 2, u % 2, b, u > 0 and b in (0, 3))
+            for a, c in {3: ((0, 8),), 7: ((8, 16),)}.get(b, ()) if n < 88 else {3: ((0, 8),), 5: ((8, 12),), 7: ((12, 16),)}.get(b, ()):
                 store(u // 4, u // 2 % 2, u % 2, a, c)
 
         nc.vector.tensor_copy(out=bias_row[0:1, :], in_=bias_in[:])
-        prepare_w(0, SV, 1, "y")
-        tick()
-        prepare_x(0, 0, SV, 1)
-        tick()
-        prepare_x(0, 1, SV, 1, "y")
+        prepare_w(0, SV, "y")
+        quantise_next()
+        prepare_x(0, 0, SV)
+        quantise_next()
+        prepare_x(0, 1, SV, "y")
         bias_everywhere(0, 1)
-        bias_everywhere(1, 1)
         tick()
-        quantise_eye()
+        quantise_next()
         bank(0)
         bank(1)
-        prepare_x(0, 2, SS, 1)
-        tick()
+        prepare_x(0, 2, SS)
+        quantise_next()
         bank(2)
         bank(3)
-        prepare_x(0, 3, SS, 1)
+        bias_everywhere(1, 1)
+        prepare_x(0, 3, SS)
+        quantise_next()
         tick()
 
-        preps = {5: (1, 0), 13: (1, 1), 17: (1, 2), 21: (1, 3), 30: (2, 0), 36: (2, 1), 42: (2, 2), 48: (2, 3)}
+        preps = {8: (1, 0), 12: (1, 1), 19: (1, 2), 27: (1, 3), 35: (2, 0), 43: (2, 1), 51: (2, 2), 59: (2, 3)}
         m_list = [(g, kb, q) for g in range(FAMILIES) for kb in range(4) for q in range(8)]
         wb_list = [(kv, kb) for kv in range(2) for kb in range(4)]
-        pause = 0
         for n in range(4, 12 * BANKS):
-            if n + 3 in preps and preps[n + 3] in ():
-                sort_words(*preps[n + 3])
-            if n == 9:
-                prepare_w(1, SS, 3)
+            if n + 6 in preps and preps[n + 6] in ((1, 1), (1, 2), (1, 3), (2, 0), (2, 1), (2, 2), (2, 3)):
+                sort_words(*preps[n + 6])
+            if n == 5:
+                prepare_w(1, SS)
             elif n in preps:
-                prepare_x(preps[n][0], preps[n][1], SS, 5)
+                prepare_x(preps[n][0], preps[n][1], SS)
             bank(n)
-            if n >= 10:
-                ready = 32 if n < 30 else 64 if n < 56 else 96
-                take = 1 if n < 48 else 2
-                while take and m_list and 96 - len(m_list) < ready and n >= pause:
+            for m in range(1 if n < 64 else 2):
+                if m_list and n >= (10, 32, 64)[m_list[0][0]]:
                     m_pass(*m_list[0])
                     m_list = m_list[1:]
-                    take -= 1
-                    if len(m_list) % 8 == 0:
-                        pause = n + 0
-            if n >= 54 and n % 3 == 0 and wb_list:
+            if n >= 37 and n % 8 in (5, 7) and wb_list:
                 weight_back(*wb_list[0])
                 wb_list = wb_list[1:]
+            if n == 5:
+                quantise_eye()
+            if n in (7, 14, 15, 23, 31, 39, 47, 55, 63):
+                quantise_next()
             tick()
-            if n == 81:
+            if n == 86:
                 split_sums()
-            if 81 + 3 <= n < 81 + 7:
-                f_block(2 * (n - 81 - 3))
-                f_block(2 * (n - 81 - 3) + 1)
-            if n in (81 + 9, 81 + 11):
-                means_out((n - 81 - 9) // 2)
+            if 86 + 3 <= n < 86 + 7:
+                f_block(2 * (n - 86 - 3))
+                f_block(2 * (n - 86 - 3) + 1)
+            if n in (86 + 8, 86 + 9):
+                means_out(n - 86 - 8)
         for n in range(4):
             tick()

@@ -277,8 +277,8 @@ def tile_chunkedattention_pb_t_kernel(
 
         def bank(n):
             u, b = n // BANKS, n % BANKS
-            y_bank(u // 4, u // 2 % 2, u % 2, b, u > 0 and b in (0, 3))
-            for a, c in {3: ((0, 8),), 7: ((8, 16),)}.get(b, ()) if n < 88 else {3: ((0, 8),), 5: ((8, 12),), 7: ((12, 16),)}.get(b, ()):
+            y_bank(u // 4, u // 2 % 2, u % 2, b, u > 0 and b in ((0, 2, 4) if u >= 8 else (0, 3)))
+            for a, c in {3: ((0, 8),), 7: ((8, 16),)}.get(b, ()) if u < 4 else {7: ((0, 16),)}.get(b, ()) if n < 80 else {3: ((0, 8),), 5: ((8, 12),), 7: ((12, 16),)}.get(b, ()):
                 store(u // 4, u // 2 % 2, u % 2, a, c)
 
         nc.vector.tensor_copy(out=bias_row[0:1, :], in_=bias_in[:])
@@ -301,7 +301,7 @@ def tile_chunkedattention_pb_t_kernel(
         quantise_next()
         tick()
 
-        preps = {8: (1, 0), 12: (1, 1), 19: (1, 2), 27: (1, 3), 35: (2, 0), 43: (2, 1), 51: (2, 2), 59: (2, 3)}
+        preps = {8: (1, 0), 15: (1, 1), 19: (1, 2), 27: (1, 3), 35: (2, 0), 43: (2, 1), 51: (2, 2), 59: (2, 3)}
         m_list = [(g, kb, q) for g in range(FAMILIES) for kb in range(4) for q in range(8)]
         wb_list = [(kv, kb) for kv in range(2) for kb in range(4)]
         for n in range(4, 12 * BANKS):
@@ -321,7 +321,7 @@ def tile_chunkedattention_pb_t_kernel(
                 wb_list = wb_list[1:]
             if n == 5:
                 quantise_eye()
-            if n in (7, 14, 15, 23, 31, 39, 47, 55, 63):
+            if n in (7, 15, 19, 23, 31, 39, 47, 55, 63):
                 quantise_next()
             tick()
             if n == 86:

@@ -34,7 +34,7 @@ def tile_chunkedattention_pb_t_kernel(
         ctx.enter_context(tc.manual_schedule())
 
         hs = hidden_states.rearrange("b (g p j) e -> (b g) p j e", p=P, j=16)
-        w_dram = [w.rearrange("(ob p) e -> p ob e", p=P) for w in (wk, wv)]
+        w_dram = [w.rearrange("(b p s) e -> p b s e", b=2, s=2) for w in (wk, wv)]
         b_dram = [b.rearrange("(o n) -> o n", o=1) for b in (bk, bv)]
         y_dram = [
             o.rearrange("b h c t d -> (b h) (c t d)").rearrange("h (g p r) -> g p h r", g=FAMILIES, p=P)
@@ -51,7 +51,7 @@ def tile_chunkedattention_pb_t_kernel(
         eye_in = const.tile([P, 2048], BF16, name="eye_in", align_bytes=64)
         eye_codes = const.tile([P, 512], U32, name="eye_codes", align_bytes=64)
         eye_scales = const.tile([P, 512], U8, name="eye_scales", align_bytes=64)
-        w_sb = [const.tile([P, 4, 512], BF16, name="w_sb%d" % kv) for kv in range(2)]
+        w_sb = [const.tile([P, 2, 2, 512], BF16, name="w_sb%d" % kv) for kv in range(2)]
         w_codes = [const.tile([P, 512], U32, name="w_codes%d" % kv, align_bytes=64) for kv in range(2)]
         w_scales = [const.tile([P, 512], U8, name="w_scales%d" % kv, align_bytes=64) for kv in range(2)]
         wt = [const.tile([P, 4, 512], BF16, name="wt%d" % kv) for kv in range(2)]
@@ -114,35 +114,34 @@ def tile_chunkedattention_pb_t_kernel(
             waiting[0]()
             waiting.remove(waiting[0])
 
-        def prepare(words, codes, scales, copies, tag="t"):
+        def prepare(words, codes, scales, copies, order, tag):
             grouped = stage.tile([P, 2048], BF16, name="grouped", align_bytes=64)
-            view = grouped[:].bitcast(F32).rearrange("q (s t u) -> q s t u", s=4, u=2)
+            view = grouped[:].bitcast(F32).rearrange("q (b r) -> q b r", b=2)
             for b in range(2):
                 bank = psum.tile([P, 2, 2, P], F32, name="bank", tag=tag, bufs=T_BUFS if tag == "t" else Y_BUFS)
                 for s in range(2):
                     for u in range(2):
                         nc.tensor.transpose(bank[:, s, u, :], words(2 * b + s, u), ident_f[:])
-                copies[b](out=view[:, 2 * b : 2 * b + 2], in_=bank[:].rearrange("q s u t -> q s t u"))
+                copies[b](
+                    out=view[:, b].rearrange("q (" + order + ") -> q " + order, u=2, t=P),
+                    in_=bank[:].rearrange("q s u t -> q " + order),
+                )
             waiting.append(lambda: nc.vector.quantize_mx(out=codes.bitcast(FP8X4), scales=scales, in_=grouped[:]))
 
         def prepare_w(kv, copies, tag="t"):
             words = w_sb[kv][:].bitcast(F32)
-            prepare(lambda s, u: words[:, s, u : 256 : 2], w_codes[kv][:], w_scales[kv][:], copies, tag)
+            part = lambda s, u: words[:, s // 2, s % 2, u : 256 : 2]
+            prepare(part, w_codes[kv][:], w_scales[kv][:], copies, "t s u", tag)
 
         def prepare_x(g, r, copies, tag="t"):
             words = x_sb[g][:].bitcast(F32)
             cols = slice(512 * r, 512 * r + 512)
             if (g, r) in sorted_words:
                 words = sorted_words[(g, r)]
-                prepare(lambda s, u: words[:, s, u, :], x_codes[g][:, cols], x_scales[g][:, cols], copies, tag)
+                part = lambda s, u: words[:, s, u, :]
             else:
-                prepare(
-                    lambda s, u: words[:, 4 * r + s, u : 256 : 2],
-                    x_codes[g][:, cols],
-                    x_scales[g][:, cols],
-                    copies,
-                    tag,
-                )
+                part = lambda s, u: words[:, 4 * r + s, u : 256 : 2]
+            prepare(part, x_codes[g][:, cols], x_scales[g][:, cols], copies, "s t u", tag)
 
         sorted_words = {}
 
@@ -277,8 +276,8 @@ def tile_chunkedattention_pb_t_kernel(
 
         def bank(n):
             u, b = n // BANKS, n % BANKS
-            y_bank(u // 4, u // 2 % 2, u % 2, b, u > 0 and b in ((0, 2, 4) if u >= 8 else (0, 3)))
-            for a, c in {3: ((0, 8),), 7: ((8, 16),)}.get(b, ()) if u < 4 else {7: ((0, 16),)}.get(b, ()) if n < 80 else {3: ((0, 8),), 5: ((8, 12),), 7: ((12, 16),)}.get(b, ()):
+            y_bank(u // 4, u // 2 % 2, u % 2, b, u > 0 and b in (1, 4))
+            for a, c in {3: ((0, 8),), 7: ((8, 16),)}.get(b, ()) if n < 88 else {3: ((0, 8),), 5: ((8, 12),), 7: ((12, 16),)}.get(b, ()):
                 store(u // 4, u // 2 % 2, u % 2, a, c)
 
         nc.vector.tensor_copy(out=bias_row[0:1, :], in_=bias_in[:])
@@ -301,7 +300,7 @@ def tile_chunkedattention_pb_t_kernel(
         quantise_next()
         tick()
 
-        preps = {8: (1, 0), 15: (1, 1), 19: (1, 2), 27: (1, 3), 35: (2, 0), 43: (2, 1), 51: (2, 2), 59: (2, 3)}
+        preps = {8: (1, 0), 14: (1, 1), 19: (1, 2), 27: (1, 3), 35: (2, 0), 43: (2, 1), 51: (2, 2), 59: (2, 3)}
         m_list = [(g, kb, q) for g in range(FAMILIES) for kb in range(4) for q in range(8)]
         wb_list = [(kv, kb) for kv in range(2) for kb in range(4)]
         for n in range(4, 12 * BANKS):

from contextlib import ExitStack

import concourse.mybir as mybir
from concourse.masks import make_identity

FLOPS = 2 * 6144 * 512 * 1024

F32 = mybir.dt.float32
BF16 = mybir.dt.bfloat16
U32 = mybir.dt.uint32
U8 = mybir.dt.uint8
FP8X4 = mybir.dt.float8_e4m3fn_x4
ADD = mybir.AluOpType.add
SUB = mybir.AluOpType.subtract
MULT = mybir.AluOpType.mult

P = 128
FAMILIES = 3
Y_BUFS = 4
T_BUFS = 2
M_BUFS = 2
BANKS = 8


def tile_chunkedattention_pb_t_kernel(
    tc, hidden_states, wk, bk, wv, bv, out_0, out_1, out_2, out_3
):
    nc = tc.nc
    with ExitStack() as ctx:
        const = ctx.enter_context(tc.tile_pool(name="const", bufs=1))
        stage = ctx.enter_context(tc.tile_pool(name="stage", bufs=3))
        ypool = ctx.enter_context(tc.tile_pool(name="ypool", bufs=5))
        psum = ctx.enter_context(tc.psum_pool(name="psum", bufs=2))
        ctx.enter_context(tc.manual_schedule())

        hs = hidden_states.rearrange("b (g p j) e -> (b g) p j e", p=P, j=16)
        w_dram = [w.rearrange("(b p s) e -> p b s e", b=2, s=2) for w in (wk, wv)]
        b_dram = [b.rearrange("(o n) -> o n", o=1) for b in (bk, bv)]
        y_dram = [
            o.rearrange("b h c t d -> (b h) (c t d)").rearrange("h (g p r) -> g p h r", g=FAMILIES, p=P)
            for o in (out_0, out_1)
        ]
        mean_dram = [o.rearrange("b h c d -> (b c) h d") for o in (out_2, out_3)]

        ident_f = const.tile([P, P], F32, name="ident_f")
        ident_b = const.tile([P, P], BF16, name="ident_b")
        ones = const.tile([P, P], BF16, name="ones")
        bias_in = const.tile([1, 1024], BF16, name="bias_in")
        bias_row = const.tile([P, 1024], BF16, name="bias_row")
        bias_bc = const.tile([P, 2, 4, P], F32, name="bias_bc")
        eye_in = const.tile([P, 2048], BF16, name="eye_in", align_bytes=64)
        eye_codes = const.tile([P, 512], U32, name="eye_codes", align_bytes=64)
        eye_scales = const.tile([P, 512], U8, name="eye_scales", align_bytes=64)
        w_sb = [const.tile([P, 2, 2, 512], BF16, name="w_sb%d" % kv) for kv in range(2)]
        w_codes = [const.tile([P, 512], U32, name="w_codes%d" % kv, align_bytes=64) for kv in range(2)]
        w_scales = [const.tile([P, 512], U8, name="w_scales%d" % kv, align_bytes=64) for kv in range(2)]
        wt = [const.tile([P, 4, 512], BF16, name="wt%d" % kv) for kv in range(2)]
        x_sb = [const.tile([P, 16, 512], BF16, name="x_sb%d" % g) for g in range(FAMILIES)]
        x_codes = [const.tile([P, 2048], U32, name="x_codes%d" % g, align_bytes=64) for g in range(FAMILIES)]
        x_scales = [const.tile([P, 2048], U8, name="x_scales%d" % g, align_bytes=64) for g in range(FAMILIES)]
        red = const.tile([P, 4, 48], F32, name="red")
        parts = const.tile([P, 4, 3, 48], BF16, name="parts")
        sums = const.tile([P, 8, P], F32, name="sums")
        rest = const.tile([P, 2, 4, 48], F32, name="rest")
        mean_sb = [const.tile([P, 4, P], F32, name="mean_sb%d" % kv) for kv in range(2)]

        state = {"clock": 0, "pending": []}

        def later(lag, fn):
            state["pending"].append((state["clock"] + lag, fn))

        def tick():
            state["clock"] += 1
            due = [x for x in state["pending"] if x[0] <= state["clock"]]
            state["pending"] = [x for x in state["pending"] if x[0] > state["clock"]]
            for x in due:
                x[1]()

        for kv in range(2):
            nc.scalar.dma_start(out=bias_in[0:1, 512 * kv : 512 * kv + 512], in_=b_dram[kv])

        def load_x(g, a, b):
            nc.sync.dma_start(out=x_sb[g][:, a:b, :], in_=hs[g][:, a:b, :])

        nc.sync.dma_start(out=w_sb[0][:], in_=w_dram[0])
        for r in range(4):
            load_x(0, 4 * r, 4 * r + 4)
        nc.sync.dma_start(out=w_sb[1][:], in_=w_dram[1])
        for g in (1, 2):
            load_x(g, 0, 8)
            load_x(g, 8, 16)

        nc.vector.memset(bias_row[:], 0.0)
        nc.vector.memset(ones[:], 1.0)
        nc.vector.memset(eye_in[:], 0.0)
        make_identity(nc, ident_f[:])
        make_identity(nc, ident_b[:])
        for a in range(4):
            nc.gpsimd.tensor_copy(
                out=eye_in[:].rearrange("p (q a b) -> p q a b", a=4, b=4)[:, :, a, a], in_=ident_b[:]
            )
        nc.gpsimd.memset(sums[:], 0.0)

        def bias_everywhere(kv, lag):
            bb_ps = psum.tile([P, 512], F32, name="bb_ps", tag="m", bufs=M_BUFS)
            nc.tensor.matmul(
                out=bb_ps[:], lhsT=ones[:], rhs=bias_row[:, 512 * kv : 512 * kv + 512], start=True, stop=True
            )
            later(lag, lambda: nc.scalar.copy(out=bias_bc[:, kv].rearrange("p h d -> p (h d)"), in_=bb_ps[:]))

        waiting = []

        def quantise_next():
            waiting[0]()
            waiting.remove(waiting[0])

        def prepare(words, codes, scales, copies, order, tag):
            grouped = stage.tile([P, 2048], BF16, name="grouped", align_bytes=64)
            view = grouped[:].bitcast(F32).rearrange("q (b r) -> q b r", b=2)
            for b in range(2):
                bank = psum.tile([P, 2, 2, P], F32, name="bank", tag=tag, bufs=T_BUFS if tag == "t" else Y_BUFS)
                for s in range(2):
                    for u in range(2):
                        nc.tensor.transpose(bank[:, s, u, :], words(2 * b + s, u), ident_f[:])
                copies[b](
                    out=view[:, b].rearrange("q (" + order + ") -> q " + order, u=2, t=P),
                    in_=bank[:].rearrange("q s u t -> q " + order),
                )
            waiting.append(lambda: nc.vector.quantize_mx(out=codes.bitcast(FP8X4), scales=scales, in_=grouped[:]))

        def prepare_w(kv, copies, tag="t"):
            words = w_sb[kv][:].bitcast(F32)
            part = lambda s, u: words[:, s // 2, s % 2, u : 256 : 2]
            prepare(part, w_codes[kv][:], w_scales[kv][:], copies, "t s u", tag)

        def prepare_x(g, r, copies, tag="t"):
            words = x_sb[g][:].bitcast(F32)
            cols = slice(512 * r, 512 * r + 512)
            if (g, r) in sorted_words:
                words = sorted_words[(g, r)]
                part = lambda s, u: words[:, s, u, :]
            else:
                part = lambda s, u: words[:, 4 * r + s, u : 256 : 2]
            prepare(part, x_codes[g][:, cols], x_scales[g][:, cols], copies, "s t u", tag)

        sorted_words = {}

        def sort_words(g, r):
            t = stage.tile([P, 4, 2, P], F32, name="sorted", bufs=2)
            sorted_words[(g, r)] = t
            nc.scalar.copy(
                out=t[:], in_=x_sb[g][:].bitcast(F32)[:, 4 * r : 4 * r + 4, :].rearrange("p s (q u) -> p s u q", u=2)
            )

        SS = (nc.scalar.copy, nc.scalar.copy)
        SV = (nc.scalar.copy, nc.vector.tensor_copy)

        units = {}

        def y_bank(g, kv, hh, b, on_scalar):
            key = (g, kv, hh)
            if key not in units:
                units[key] = ypool.tile([P, 2, 16, P], F32, name="yb")
            y_ps = psum.tile([P, 2, 256], F32, name="y_ps", tag="y", bufs=Y_BUFS)
            feats = slice(256 * hh, 256 * hh + 256)
            for s in range(2):
                toks = slice(P * (2 * b + s), P * (2 * b + s) + P)
                nc.tensor.matmul_mx(
                    out=y_ps[:, s, :],
                    lhsT=x_codes[g][:, toks].bitcast(FP8X4),
                    lhsT_scale=x_scales[g][:, toks],
                    rhs=w_codes[kv][:, feats].bitcast(FP8X4),
                    rhs_scale=w_scales[kv][:, feats],
                    start=True,
                    stop=True,
                )
            dst = units[key][:, :, 2 * b : 2 * b + 2, :].rearrange("p h j d -> p j h d")
            src = y_ps[:].rearrange("p j (h d) -> p j h d", h=2)
            bias = bias_bc[:, kv, 2 * hh : 2 * hh + 2, :].unsqueeze(1).to_broadcast([P, 2, 2, P])
            if on_scalar:
                nc.scalar.copy(out=dst, in_=src)
                nc.gpsimd.tensor_tensor(out=dst, in0=dst, in1=bias, op=ADD)
            else:
                nc.vector.tensor_tensor(out=dst, in0=src, in1=bias, op=ADD)

        def store(g, kv, hh, a, b):
            nc.sync.dma_start(
                out=y_dram[kv][g][:, 2 * hh : 2 * hh + 2, :].rearrange("p h (j d) -> p h j d", d=P)[:, :, a:b, :],
                in_=units[(g, kv, hh)][:, :, a:b, :],
            )

        m_tiles = {}

        def quantise_eye():
            nc.vector.quantize_mx(out=eye_codes[:].bitcast(FP8X4), scales=eye_scales[:], in_=eye_in[:])

        def m_pass(g, kb, q):
            if q == 0:
                m_tiles[(g, kb)] = psum.tile([P, 256], F32, name="m_ps", tag="m", bufs=M_BUFS)
            m_ps = m_tiles[(g, kb)]
            toks = slice(256 * q, 256 * q + 256)
            ks = slice(P * kb, P * kb + P)
            nc.tensor.matmul_mx(
                out=m_ps[:],
                lhsT=eye_codes[:, ks].bitcast(FP8X4),
                lhsT_scale=eye_scales[:, ks],
                rhs=x_codes[g][:, toks].bitcast(FP8X4),
                rhs_scale=x_scales[g][:, toks],
                start=(q == 0),
                stop=(q == 7),
            )
            if q == 7:
                later(
                    1,
                    lambda: nc.vector.tensor_reduce(
                        out=red[:, kb, 16 * g : 16 * g + 16],
                        in_=m_ps[:].rearrange("d (s c p) -> d c s p", s=2, p=8),
                        axis=mybir.AxisListType.XY,
                        op=ADD,
                    ),
                )

        def weight_back(kv, kb):
            ks = slice(P * kb, P * kb + P)
            wt_ps = psum.tile([P, 512], F32, name="wt_ps", tag="t", bufs=T_BUFS)
            nc.tensor.matmul_mx(
                out=wt_ps[:],
                lhsT=eye_codes[:, ks].bitcast(FP8X4),
                lhsT_scale=eye_scales[:, ks],
                rhs=w_codes[kv][:].bitcast(FP8X4),
                rhs_scale=w_scales[kv][:],
                start=True,
                stop=True,
            )
            later(1, lambda: nc.scalar.copy(out=wt[kv][:, kb, :], in_=wt_ps[:]))

        def split_sums():
            nc.vector.tensor_copy(out=parts[:, :, 0, :], in_=red[:])
            nc.vector.tensor_tensor(out=rest[:, 0], in0=red[:], in1=parts[:, :, 0, :], op=SUB)
            nc.vector.tensor_copy(out=parts[:, :, 1, :], in_=rest[:, 0])
            nc.vector.tensor_tensor(out=rest[:, 1], in0=rest[:, 0], in1=parts[:, :, 1, :], op=SUB)
            nc.vector.tensor_copy(out=parts[:, :, 2, :], in_=rest[:, 1])

        def f_block(fb):
            if fb == 0:
                m_tiles["f"] = psum.tile([P, 8, 48], F32, name="f_ps", tag="m", bufs=M_BUFS)
            f_ps = m_tiles["f"]
            for n in range(12):
                nc.tensor.matmul(
                    out=f_ps[:, fb, :],
                    lhsT=wt[fb // 4][:, n % 4, P * (fb % 4) : P * (fb % 4) + P],
                    rhs=parts[:, n % 4, n // 4, :],
                    start=(n == 0),
                    stop=(n == 11),
                )
            if fb == 7:
                later(1, lambda: nc.scalar.copy(out=sums[:, :, 0:48], in_=f_ps[:]))

        def means_out(kv):
            t_ps = psum.tile([P, 4, P], F32, name="t_ps", tag="t", bufs=T_BUFS)
            for h in range(4):
                nc.tensor.transpose(t_ps[:, h, :], sums[:, 4 * kv + h, :], ident_f[:])

            def finish():
                nc.vector.scalar_tensor_tensor(
                    out=mean_sb[kv][0:48].rearrange("c h d -> c (h d)"),
                    in0=t_ps[0:48].rearrange("c h d -> c (h d)"),
                    scalar=1.0 / 128.0,
                    in1=bias_bc[0:48, kv].rearrange("c h d -> c (h d)"),
                    op0=MULT,
                    op1=ADD,
                )
                nc.sync.dma_start(out=mean_dram[kv], in_=mean_sb[kv][0:48])

            later(1, finish)

        def bank(n):
            u, b = n // BANKS, n % BANKS
            y_bank(u // 4, u // 2 % 2, u % 2, b, u > 0 and b in (1, 4))
            for a, c in {3: ((0, 8),), 7: ((8, 16),)}.get(b, ()) if n < 88 else {3: ((0, 8),), 5: ((8, 12),), 7: ((12, 16),)}.get(b, ()):
                store(u // 4, u // 2 % 2, u % 2, a, c)

        nc.vector.tensor_copy(out=bias_row[0:1, :], in_=bias_in[:])
        prepare_w(0, SV, "y")
        quantise_next()
        prepare_x(0, 0, SV)
        quantise_next()
        prepare_x(0, 1, SV, "y")
        bias_everywhere(0, 1)
        tick()
        quantise_next()
        bank(0)
        bank(1)
        prepare_x(0, 2, SS)
        quantise_next()
        bank(2)
        bank(3)
        bias_everywhere(1, 1)
        prepare_x(0, 3, SS)
        quantise_next()
        tick()

        preps = {8: (1, 0), 14: (1, 1), 19: (1, 2), 27: (1, 3), 35: (2, 0), 43: (2, 1), 51: (2, 2), 59: (2, 3)}
        m_list = [(g, kb, q) for g in range(FAMILIES) for kb in range(4) for q in range(8)]
        wb_list = [(kv, kb) for kv in range(2) for kb in range(4)]
        for n in range(4, 12 * BANKS):
            if n + 6 in preps and preps[n + 6] in ((1, 1), (1, 2), (1, 3), (2, 0), (2, 1), (2, 2), (2, 3)):
                sort_words(*preps[n + 6])
            if n == 5:
                prepare_w(1, SS)
            elif n in preps:
                prepare_x(preps[n][0], preps[n][1], SS)
            bank(n)
            for m in range(1 if n < 64 else 2):
                if m_list and n >= (10, 32, 64)[m_list[0][0]]:
                    m_pass(*m_list[0])
                    m_list = m_list[1:]
            if n >= 37 and n % 8 in (5, 7) and wb_list:
                weight_back(*wb_list[0])
                wb_list = wb_list[1:]
            if n == 5:
                quantise_eye()
            if n in (7, 15, 19, 23, 31, 39, 47, 55, 63):
                quantise_next()
            tick()
            if n == 86:
                split_sums()
            if 86 + 3 <= n < 86 + 7:
                f_block(2 * (n - 86 - 3))
                f_block(2 * (n - 86 - 3) + 1)
            if n in (86 + 8, 86 + 9):
                means_out(n - 86 - 8)
        for n in range(4):
            tick()
